import numpy as np
import ml_dtypes


def mxq(x, axis, fmt="e4m3"):
    dtype, down = {"e4m3": (ml_dtypes.float8_e4m3fn, 7), "e5m2": (ml_dtypes.float8_e5m2, 14)}[fmt]
    v = np.moveaxis(np.asarray(x, np.float32).astype(ml_dtypes.bfloat16).astype(np.float64), axis, -1)
    blocks = v.reshape(v.shape[:-1] + (-1, 32))
    amax = np.abs(blocks).max(-1, keepdims=True)
    byte = np.maximum(np.where(amax > 0, np.frexp(amax)[1] - 1 + 127, 0) - down, 1)
    scale = np.exp2(byte - 127.0)
    codes = (blocks / scale).astype(np.float32).astype(dtype).astype(np.float64)
    return np.moveaxis((codes * scale).reshape(v.shape), -1, axis)


WIDE = False


def mx_kscale(k):
    if not WIDE:
        return np.ones(k)
    levels = np.array([10, -10, 5, -5, 0])
    a = np.random.permutation(np.resize(levels, k // 512 * 4)).reshape(k // 512, 4)
    idx = np.arange(k)
    return np.exp2(a[idx // 512, idx % 128 // 32])


BF16 = ml_dtypes.bfloat16


def bf(x):
    return np.asarray(x, np.float32).astype(BF16)


def f64(x):
    return np.asarray(x).astype(np.float64)


T, B, C, E, H = 256, 2, 768, 2048, 16
D = E // H
S = C + T
NEG_INF = -10000000000.0


def setup_inputs():
    s = mx_kscale(E)
    return {
        "x": bf(np.random.standard_normal((T, B, E)) * s),
        "q": bf(np.random.standard_normal((T, B, E)) * 2.0 / np.sqrt(D)),
        "k_new": bf(np.random.standard_normal((T, B, E))),
        "cache_k": bf(np.random.standard_normal((B * H, C, D))),
        "cache_v": bf(np.random.standard_normal((B * H, C, D))),
        "Wv": bf(np.random.standard_normal((E, E)) / np.sqrt(E) / s[None, :]),
        "bv": bf(np.random.standard_normal(E) * 0.3),
    }


def reference(x, q, k_new, cache_k, cache_v, Wv, bv):
    v_new = (mxq(f64(x), 2, "e4m3") @ mxq(f64(Wv), 1, "e4m3").T) + f64(bv)
    vh = v_new.reshape(T, B * H, D).transpose(1, 0, 2)
    qh = f64(q).reshape(T, B * H, D).transpose(1, 0, 2)
    kh = f64(k_new).reshape(T, B * H, D).transpose(1, 0, 2)
    causal = np.triu(np.full((T, T), NEG_INF), k=1)
    s_cache = qh @ f64(cache_k).transpose(0, 2, 1)
    s_new = qh @ kh.transpose(0, 2, 1)
    s = np.concatenate([s_cache, s_new + causal[None, :, :]], axis=2)
    e = np.exp(s - s.max(-1, keepdims=True))
    v = np.concatenate([f64(cache_v), vh], axis=1)
    attn = (mxq(e, 2, "e4m3") @ mxq(v, 1, "e4m3")) / e.sum(-1, keepdims=True)
    merged = attn.transpose(1, 0, 2).reshape(T, B, E)
    return merged, vh

@@ -1,0 +1,472 @@
+from contextlib import ExitStack
+
+import concourse.mybir as mybir
+from concourse.masks import make_identity
+
+BF16 = mybir.dt.bfloat16
+F32 = mybir.dt.float32
+U32 = mybir.dt.uint32
+U8 = mybir.dt.uint8
+FP8X4 = mybir.dt.float8_e4m3fn_x4
+ALU = mybir.AluOpType
+ACT = mybir.ActivationFunctionType
+AXIS_X = mybir.AxisListType.X
+
+T, B, C, E, H = 256, 2, 768, 2048, 16
+D = E // H
+S = C + T
+NEG_INF = -10000000000.0
+
+P = 128
+K_PASS = 4 * P
+PROJ_PASSES = E // K_PASS
+KEY_PASSES = S // K_PASS
+BANK = 512
+Q_TILES = T // P
+CACHE_TILES = C // P
+BLOCK_FEATS = 2 * D
+BLOCKS = E // BLOCK_FEATS
+BLOCK_HEADS = 2 * B
+HEADS = BLOCKS * BLOCK_HEADS
+STEPS = HEADS * Q_TILES
+BLOCK_STEPS = BLOCK_HEADS * Q_TILES
+
+FLOPS = 2 * T * B * E * E + 2 * 2 * B * H * T * S * D
+
+
+def tile_multiheadlmattentionwithcache_pa_kernel(
+    tc, x, q, k_new, cache_k, cache_v, Wv, bv, out_0, out_1
+):
+    nc = tc.nc
+    with ExitStack() as ctx:
+        consts = ctx.enter_context(tc.tile_pool(name="consts", bufs=1))
+        loads = ctx.enter_context(tc.tile_pool(name="loads", bufs=3))
+        work = ctx.enter_context(tc.tile_pool(name="work", bufs=2))
+        small = ctx.enter_context(tc.tile_pool(name="small", bufs=4))
+        psum = ctx.enter_context(tc.psum_pool(name="psum", bufs=1))
+        psum_s = ctx.enter_context(tc.psum_pool(name="psum_s", bufs=2))
+        ctx.enter_context(tc.manual_schedule())
+
+        w_rows, qk_raw, ck_raw, cv_raw = {}, {}, {}, {}
+        w_grouped, w_codes, vh, v_grouped, v_codes = {}, {}, {}, {}, {}
+        qT, kT, s_banks, neg_max, e_bf, sums = {}, {}, {}, {}, {}, {}
+        e_grouped, e_codes, recip, merged = {}, {}, {}, {}
+
+        ident_bf = consts.tile([P, P], BF16)
+        make_identity(nc, ident_bf[:])
+        ident_f32 = consts.tile([P, P], F32)
+        make_identity(nc, ident_f32[:])
+        mask_f32 = consts.tile([P, P], F32)
+        nc.gpsimd.memset(mask_f32[:], 0.0)
+        nc.gpsimd.affine_select(
+            out=mask_f32[:],
+            in_=mask_f32[:],
+            compare_op=ALU.is_ge,
+            fill=NEG_INF,
+            base=0,
+            pattern=[[-1, P]],
+            channel_multiplier=1,
+        )
+        mask_bf = consts.tile([P, P], BF16)
+        nc.vector.tensor_copy(out=mask_bf[:], in_=mask_f32[:])
+        e_first = [consts.tile([P, S], BF16, name="e_first%d" % j) for j in range(2)]
+        for j in range(2):
+            nc.vector.memset(e_first[j][:, S - P : S], 0.0)
+        bias = consts.tile([P, E], BF16)
+        x_codes = consts.tile([P, PROJ_PASSES, 4 * P], U32, align_bytes=64)
+        x_scales = consts.tile([P, PROJ_PASSES, 4 * P], U8, align_bytes=64)
+
+        def load_x(pair):
+            rows = loads.tile([P, 2, E], BF16, tag="rows", bufs=4, name="x_rows")
+            nc.sync.dma_start(
+                out=rows[:].rearrange("p b k -> p (b k)"),
+                in_=x.rearrange("(p e) b k -> e p (b k)", e=2)[pair],
+            )
+            return rows
+
+        def load_weights(block):
+            first = block * BLOCK_FEATS
+            rows = loads.tile([P, 2, E], BF16, tag="rows", bufs=4, name="w_rows")
+            nc.sync.dma_start(
+                out=rows[:],
+                in_=Wv[first : first + BLOCK_FEATS, :].rearrange("(r p) k -> p r k", p=P),
+            )
+            w_rows[block] = rows
+
+        def load_queries_keys(two_blocks):
+            feats = slice(two_blocks * BANK, (two_blocks + 1) * BANK)
+            q_raw = loads.tile([P, Q_TILES, B, BANK], BF16, bufs=2, name="q_raw")
+            k_raw = loads.tile([P, Q_TILES, B, BANK], BF16, bufs=2, name="k_raw")
+            for i in range(Q_TILES):
+                rows = slice(i * P, (i + 1) * P)
+                nc.sync.dma_start(out=q_raw[:, i], in_=q[rows, :, feats])
+                nc.sync.dma_start(out=k_raw[:, i], in_=k_new[rows, :, feats])
+            qk_raw[two_blocks] = (q_raw, k_raw)
+
+        def load_cache(block):
+            ck = loads.tile([P, BLOCK_HEADS, CACHE_TILES, D], BF16, name="ck")
+            cv = loads.tile([P, BLOCK_HEADS, 3, 2, D], BF16, name="cv")
+            for b in range(B):
+                n0 = b * H + 2 * block
+                nc.sync.dma_start(
+                    out=ck[:, 2 * b : 2 * b + 2].rearrange("p n a d -> p (n a) d"),
+                    in_=cache_k[n0 : n0 + 2].rearrange("n (a p) d -> p (n a) d", p=P),
+                )
+            for b in range(B):
+                n0 = b * H + 2 * block
+                nc.sync.dma_start(
+                    out=cv[:, 2 * b : 2 * b + 2].rearrange("p n c e d -> p (n c) (e d)"),
+                    in_=cache_v[n0 : n0 + 2].rearrange("n (c p e) d -> p (n c) (e d)", c=3, e=2),
+                )
+            ck_raw[block] = ck
+            cv_raw[block] = cv
+
+        def transpose_rows(rows, g, bank_pool, bank_tag, copy_out):
+            words = (
+                rows[:]
+                .rearrange("p r k -> p (r k)")
+                .bitcast(F32)
+                .rearrange("p (r w) -> p r w", r=2)
+            )
+            bank = bank_pool.tile([P, 2, 2, P], F32, tag=bank_tag, name="rows_T")
+            for r in range(2):
+                for u in range(2):
+                    first = (2 * g + u) * P
+                    nc.tensor.transpose(bank[:, r, u, :], words[:, r, first : first + P], ident_f32[:])
+            grouped = work.tile(
+                [P, 2, P, 2], F32, tag="rows_grouped", bufs=3, align_bytes=64, name="rows_grouped"
+            )
+            copy_out(out=grouped[:], in_=bank[:].rearrange("p r u c -> p r c u"))
+            return grouped
+
+        def quantise_rows(grouped, codes, scales):
+            nc.vector.quantize_mx(
+                out=codes.bitcast(FP8X4),
+                scales=scales,
+                in_=grouped[:].rearrange("p r c u -> p (r c u)").bitcast(BF16),
+            )
+
+        def transpose_weights(block, g):
+            if block < BLOCKS:
+                w_grouped[block, g] = transpose_rows(
+                    w_rows[block], g, psum, "proj", nc.vector.tensor_copy
+                )
+
+        def quantise_weights(block, g):
+            if block < BLOCKS:
+                if g == 0:
+                    codes = work.tile([P, PROJ_PASSES, BLOCK_FEATS], U32, align_bytes=64, name="w_codes")
+                    scales = work.tile([P, PROJ_PASSES, BLOCK_FEATS], U8, align_bytes=64, name="w_scales")
+                    w_codes[block] = (codes, scales)
+                codes, scales = w_codes[block]
+                quantise_rows(w_grouped[block, g], codes[:, g, :], scales[:, g, :])
+
+        def regroup_cache(block):
+            if block < BLOCKS:
+                grouped = work.tile([P, BLOCK_HEADS, KEY_PASSES, D, 4], BF16, align_bytes=64, name="v_grouped")
+                nc.gpsimd.tensor_scalar(
+                    out=grouped[:, :, 0, :, :],
+                    in0=cv_raw[block][:, :, 0:2, :, :].rearrange("p n c e d -> p n d (c e)"),
+                    scalar1=1.0,
+                    scalar2=0.0,
+                    op0=ALU.mult,
+                    op1=ALU.add,
+                )
+                nc.gpsimd.tensor_scalar(
+                    out=grouped[:, :, 1, :, 0:2],
+                    in0=cv_raw[block][:, :, 2, :, :].rearrange("p n e d -> p n d e"),
+                    scalar1=1.0,
+                    scalar2=0.0,
+                    op0=ALU.mult,
+                    op1=ALU.add,
+                )
+                v_grouped[block] = grouped
+
+        def project(block, e, b):
+            if e == 0 and b == 0:
+                vh[block] = work.tile([P, BLOCK_HEADS, 2, D], F32, name="vh")
+            codes, scales = w_codes[block]
+            tokens = slice((2 * e + b) * P, (2 * e + b + 1) * P)
+            first = block * BLOCK_FEATS
+            acc = psum.tile([P, BLOCK_FEATS], F32, tag="proj", name="acc")
+            for g in range(PROJ_PASSES):
+                nc.tensor.matmul_mx(
+                    out=acc[:],
+                    lhsT=x_codes[:, g, tokens].bitcast(FP8X4),
+                    lhsT_scale=x_scales[:, g, tokens],
+                    rhs=codes[:, g, :].bitcast(FP8X4),
+                    rhs_scale=scales[:, g, :],
+                    start=(g == 0),
+                    stop=(g == PROJ_PASSES - 1),
+                )
+            pair = slice(2 * b, 2 * b + 2)
+            nc.vector.tensor_tensor(
+                out=vh[block][:, pair, e, :],
+                in0=acc[:].rearrange("p (n d) -> p n d", d=D),
+                in1=bias[:, first : first + BLOCK_FEATS].rearrange("p (n d) -> p n d", d=D),
+                op=ALU.add,
+            )
+            if e == 1:
+                n0 = b * H + 2 * block
+                nc.sync.dma_start(
+                    out=out_1[n0 : n0 + 2].rearrange("n (p e) d -> p n (e d)", e=2),
+                    in_=vh[block][:, pair].rearrange("p n e d -> p n (e d)"),
+                )
+                nc.gpsimd.tensor_scalar(
+                    out=v_grouped[block][:, pair, 1, :, 2:4],
+                    in0=vh[block][:, pair].rearrange("p n e d -> p n d e"),
+                    scalar1=1.0,
+                    scalar2=0.0,
+                    op0=ALU.mult,
+                    op1=ALU.add,
+                )
+
+        def quantise_v(block, b):
+            if b == 0:
+                codes = work.tile([P, BLOCK_HEADS, KEY_PASSES, D], U32, align_bytes=64, name="v_codes")
+                scales = work.tile([P, BLOCK_HEADS, KEY_PASSES, D], U8, align_bytes=64, name="v_scales")
+                v_codes[block] = (codes, scales)
+            codes, scales = v_codes[block]
+            pair = slice(2 * b, 2 * b + 2)
+            nc.vector.quantize_mx(
+                out=codes[:, pair].rearrange("p n g d -> p (n g d)").bitcast(FP8X4),
+                scales=scales[:, pair].rearrange("p n g d -> p (n g d)"),
+                in_=v_grouped[block][:, pair].rearrange("p n g d t -> p (n g d t)"),
+            )
+
+        def place(head):
+            block, rest = divmod(head, BLOCK_HEADS)
+            b, h = divmod(rest, 2)
+            return block, b, h
+
+        def transpose_queries(block):
+            q_raw = qk_raw[block // 2][0]
+            bank = psum.tile([P, BLOCK_HEADS, T], BF16, tag="kq", name="qT_ps")
+            for b in range(B):
+                for h in range(2):
+                    first = ((block % 2) * 2 + h) * D
+                    for i in range(Q_TILES):
+                        nc.tensor.transpose(
+                            bank[:, 2 * b + h, i * P : (i + 1) * P],
+                            q_raw[:, i, b, first : first + D],
+                            ident_bf[:],
+                        )
+            qT[block] = work.tile([P, BLOCK_HEADS, T], BF16, name="qT")
+            nc.scalar.copy(out=qT[block][:], in_=bank[:])
+
+        def transpose_keys(head):
+            block, b, h = place(head)
+            k_raw = qk_raw[block // 2][1]
+            first = ((block % 2) * 2 + h) * D
+            bank = psum.tile([P, S], BF16, tag="kq", name="kT_ps")
+            for a in range(CACHE_TILES):
+                nc.tensor.transpose(
+                    bank[:, a * P : (a + 1) * P], ck_raw[block][:, 2 * b + h, a, :], ident_bf[:]
+                )
+            for i in range(Q_TILES):
+                nc.tensor.transpose(
+                    bank[:, C + i * P : C + (i + 1) * P],
+                    k_raw[:, i, b, first : first + D],
+                    ident_bf[:],
+                )
+            kT[head] = work.tile([P, S], BF16, name="kT")
+            nc.scalar.copy(out=kT[head][:], in_=bank[:])
+
+        def seen_keys(i):
+            return C + (i + 1) * P
+
+        def scores(tile):
+            head, i = divmod(tile, Q_TILES)
+            block, b, h = place(head)
+            queries = qT[block][:, 2 * b + h, i * P : (i + 1) * P]
+            keys = kT[head]
+            seen = seen_keys(i)
+            diag = seen - P
+            s_lo = psum_s.tile([P, BANK], F32, tag="s_lo", name="s_lo")
+            s_hi = psum_s.tile([P, BANK], F32, tag="s_hi", name="s_hi")
+            nc.tensor.matmul(s_lo[:], lhsT=queries, rhs=keys[:, 0:BANK], start=True, stop=True)
+            nc.tensor.matmul(
+                s_hi[:, 0 : diag - BANK], lhsT=queries, rhs=keys[:, BANK:diag], start=True, stop=True
+            )
+            nc.tensor.matmul(
+                s_hi[:, diag - BANK : seen - BANK],
+                lhsT=queries,
+                rhs=keys[:, diag:seen],
+                start=True,
+                stop=False,
+            )
+            nc.tensor.matmul(
+                s_hi[:, diag - BANK : seen - BANK],
+                lhsT=ident_bf[:],
+                rhs=mask_bf[:],
+                start=False,
+                stop=True,
+            )
+            s_banks[tile] = (s_lo, s_hi)
+
+        def row_maxima(tile):
+            s_lo, s_hi = s_banks[tile]
+            seen = seen_keys(tile % Q_TILES)
+            maxima = small.tile([P, 2], F32, name="maxima")
+            nc.vector.tensor_reduce(out=maxima[:, 0:1], in_=s_lo[:], axis=AXIS_X, op=ALU.max)
+            nc.vector.tensor_reduce(
+                out=maxima[:, 1:2], in_=s_hi[:, 0 : seen - BANK], axis=AXIS_X, op=ALU.max
+            )
+            neg_max[tile] = small.tile([P, 1], F32, name="neg_max")
+            nc.vector.tensor_reduce(
+                out=neg_max[tile][:], in_=maxima[:], axis=AXIS_X, op=ALU.max, negate=True
+            )
+
+        def exponentials(tile):
+            head, i = divmod(tile, Q_TILES)
+            s_lo, s_hi = s_banks[tile]
+            seen = seen_keys(i)
+            if i == 0:
+                sums[head] = small.tile([P, Q_TILES, 2], F32, name="sums")
+                e_bf[tile] = e_first[head % 2]
+            else:
+                e_bf[tile] = work.tile([P, S], BF16, name="e_second")
+            nc.scalar.activation(
+                out=e_bf[tile][:, 0:BANK],
+                in_=s_lo[:],
+                func=ACT.Exp,
+                bias=neg_max[tile][:],
+                scale=1.0,
+                accum_out=sums[head][:, i, 0:1],
+            )
+            nc.scalar.activation(
+                out=e_bf[tile][:, BANK:seen],
+                in_=s_hi[:, 0 : seen - BANK],
+                func=ACT.Exp,
+                bias=neg_max[tile][:],
+                scale=1.0,
+                accum_out=sums[head][:, i, 1:2],
+            )
+
+        def transpose_e(tile):
+            head, i = divmod(tile, Q_TILES)
+            if i == 0:
+                e_grouped[head] = work.tile(
+                    [P, Q_TILES, KEY_PASSES, P, 2], F32, bufs=3, align_bytes=64, name="e_grouped"
+                )
+            e_words = e_bf[tile][:].bitcast(F32)
+            bank = psum.tile([P, 2 * KEY_PASSES, P], F32, tag="eT", name="eT_ps")
+            for w in range(2 * KEY_PASSES):
+                nc.tensor.transpose(bank[:, w, :], e_words[:, w * P : (w + 1) * P], ident_f32[:])
+            nc.scalar.copy(
+                out=e_grouped[head][:, i], in_=bank[:].rearrange("p (g u) c -> p g c u", u=2)
+            )
+
+        def quantise_e(head):
+            codes = work.tile([P, Q_TILES, KEY_PASSES, P], U32, align_bytes=64, name="e_codes")
+            scales = work.tile([P, Q_TILES, KEY_PASSES, P], U8, align_bytes=64, name="e_scales")
+            nc.vector.quantize_mx(
+                out=codes[:].rearrange("p i g c -> p (i g c)").bitcast(FP8X4),
+                scales=scales[:].rearrange("p i g c -> p (i g c)"),
+                in_=e_grouped[head][:].rearrange("p i g c u -> p (i g c u)").bitcast(BF16),
+            )
+            e_codes[head] = (codes, scales)
+            total = small.tile([P, Q_TILES], F32, name="total")
+            nc.vector.tensor_reduce(out=total[:], in_=sums[head][:], axis=AXIS_X, op=ALU.add)
+            recip[head] = small.tile([P, Q_TILES], F32, name="recip")
+            nc.vector.reciprocal(out=recip[head][:], in_=total[:])
+
+        def weighted_sum(head):
+            block, b, h = place(head)
+            if h == 0:
+                merged[block, b] = work.tile([P, Q_TILES, BLOCK_FEATS], F32, name="merged")
+            codes, scales = e_codes[head]
+            values, value_scales = v_codes[block]
+            pv = psum.tile([P, Q_TILES, D], F32, tag="pv", name="pv")
+            for i in range(Q_TILES):
+                for g in range(KEY_PASSES):
+                    nc.tensor.matmul_mx(
+                        out=pv[:, i, :],
+                        lhsT=codes[:, i, g, :].bitcast(FP8X4),
+                        lhsT_scale=scales[:, i, g, :],
+                        rhs=values[:, 2 * b + h, g, :].bitcast(FP8X4),
+                        rhs_scale=value_scales[:, 2 * b + h, g, :],
+                        start=(g == 0),
+                        stop=(g == KEY_PASSES - 1),
+                    )
+            for i in range(Q_TILES):
+                nc.scalar.activation(
+                    out=merged[block, b][:, i, h * D : (h + 1) * D],
+                    in_=pv[:, i, :],
+                    func=ACT.Copy,
+                    scale=recip[head][:, i : i + 1],
+                )
+            if h == 1:
+                first = block * BLOCK_FEATS
+                nc.sync.dma_start(
+                    out=out_0.rearrange("(i p) b f -> p i b f", p=P)[
+                        :, :, b, first : first + BLOCK_FEATS
+                    ],
+                    in_=merged[block, b][:],
+                )
+
+        x_rows = [load_x(0), load_x(1)]
+        load_weights(0)
+        load_queries_keys(0)
+        load_cache(0)
+        nc.sync.dma_start(out=bias[:], in_=bv.partition_broadcast(P))
+        load_weights(1)
+        load_cache(1)
+
+        start_grouped = {}
+        for r in range(3 * PROJ_PASSES + 1):
+            if r < 3 * PROJ_PASSES:
+                operand, g = divmod(r, PROJ_PASSES)
+                rows = x_rows[operand] if operand < 2 else w_rows[0]
+                start_grouped[r] = transpose_rows(
+                    rows, g, psum_s, ("s_lo", "s_hi")[r % 2], nc.scalar.copy
+                )
+            if r > 0:
+                operand, g = divmod(r - 1, PROJ_PASSES)
+                if operand < 2:
+                    tokens = slice(operand * 2 * P, (operand + 1) * 2 * P)
+                    quantise_rows(start_grouped[r - 1], x_codes[:, g, tokens], x_scales[:, g, tokens])
+                else:
+                    w_grouped[0, g] = start_grouped[r - 1]
+                    quantise_weights(0, g)
+        regroup_cache(0)
+        transpose_queries(0)
+
+        for k in range(-4, STEPS + 4):
+            clock = k + 3
+            if 0 <= k < STEPS:
+                exponentials(k)
+            if 0 <= k - 1 < STEPS:
+                transpose_e(k - 1)
+            if k % 2 == 1 and clock > 0:
+                quantise_weights((clock - 1) // BLOCK_STEPS + 1, ((clock - 1) % BLOCK_STEPS) // 2)
+            if 0 <= k + 1 < STEPS:
+                row_maxima(k + 1)
+            if k % 2 == 0:
+                if k // 2 + 2 < HEADS:
+                    transpose_keys(k // 2 + 2)
+                if clock > 0:
+                    transpose_weights(clock // BLOCK_STEPS + 1, (clock % BLOCK_STEPS) // 2)
+                if 0 <= k // 2 - 2 < HEADS:
+                    quantise_e(k // 2 - 2)
+            else:
+                if (k + 5) % BLOCK_STEPS == 0 and 0 < (k + 5) // BLOCK_STEPS < BLOCKS:
+                    transpose_queries((k + 5) // BLOCK_STEPS)
+                if clock // BLOCK_STEPS < BLOCKS:
+                    e, b = divmod((clock % BLOCK_STEPS) // 2, B)
+                    project(clock // BLOCK_STEPS, e, b)
+                block, late = divmod(k - 3, BLOCK_STEPS)
+                if 0 <= block < BLOCKS and late in (0, 2):
+                    quantise_v(block, late // 2)
+                if 0 <= (k - 5) // 2 < HEADS:
+                    weighted_sum((k - 5) // 2)
+            if 0 <= k + 2 < STEPS:
+                scores(k + 2)
+            if k >= 0 and k % BLOCK_STEPS == 0:
+                block = k // BLOCK_STEPS
+                regroup_cache(block + 1)
+                if block + 2 < BLOCKS:
+                    load_weights(block + 2)
+                    if block % 2 == 0:
+                        load_queries_keys(block // 2 + 1)
+                    load_cache(block + 2)

@@ -49,8 +49,8 @@ def tile_multiheadlmattentionwithcache_pa_kernel(
 
         w_rows, qk_raw, ck_raw, cv_raw = {}, {}, {}, {}
         w_grouped, w_codes, vh, v_grouped, v_codes = {}, {}, {}, {}, {}
-        qT, kT, s_banks, neg_max, e_bf, sums = {}, {}, {}, {}, {}, {}
-        e_grouped, e_codes, recip, merged = {}, {}, {}, {}
+        qT, kT, s_banks, maxima, neg_max, e_bf, sums = {}, {}, {}, {}, {}, {}, {}
+        e_grouped, e_codes, totals, recip, merged = {}, {}, {}, {}, {}
 
         ident_bf = consts.tile([P, P], BF16)
         make_identity(nc, ident_bf[:])
@@ -304,17 +304,19 @@ def tile_multiheadlmattentionwithcache_pa_kernel(
             )
             s_banks[tile] = (s_lo, s_hi)
 
-        def row_maxima(tile):
+        def bank_maxima(tile):
             s_lo, s_hi = s_banks[tile]
             seen = seen_keys(tile % Q_TILES)
-            maxima = small.tile([P, 2], F32, name="maxima")
-            nc.vector.tensor_reduce(out=maxima[:, 0:1], in_=s_lo[:], axis=AXIS_X, op=ALU.max)
+            maxima[tile] = small.tile([P, 2], F32, name="maxima")
+            nc.vector.tensor_reduce(out=maxima[tile][:, 0:1], in_=s_lo[:], axis=AXIS_X, op=ALU.max)
             nc.vector.tensor_reduce(
-                out=maxima[:, 1:2], in_=s_hi[:, 0 : seen - BANK], axis=AXIS_X, op=ALU.max
+                out=maxima[tile][:, 1:2], in_=s_hi[:, 0 : seen - BANK], axis=AXIS_X, op=ALU.max
             )
+
+        def negated_maximum(tile):
             neg_max[tile] = small.tile([P, 1], F32, name="neg_max")
             nc.vector.tensor_reduce(
-                out=neg_max[tile][:], in_=maxima[:], axis=AXIS_X, op=ALU.max, negate=True
+                out=neg_max[tile][:], in_=maxima[tile][:], axis=AXIS_X, op=ALU.max, negate=True
             )
 
         def exponentials(tile):
@@ -366,10 +368,14 @@ def tile_multiheadlmattentionwithcache_pa_kernel(
                 in_=e_grouped[head][:].rearrange("p i g c u -> p (i g c u)").bitcast(BF16),
             )
             e_codes[head] = (codes, scales)
-            total = small.tile([P, Q_TILES], F32, name="total")
-            nc.vector.tensor_reduce(out=total[:], in_=sums[head][:], axis=AXIS_X, op=ALU.add)
+
+        def row_totals(head):
+            totals[head] = small.tile([P, Q_TILES], F32, name="totals")
+            nc.vector.tensor_reduce(out=totals[head][:], in_=sums[head][:], axis=AXIS_X, op=ALU.add)
+
+        def reciprocals(head):
             recip[head] = small.tile([P, Q_TILES], F32, name="recip")
-            nc.vector.reciprocal(out=recip[head][:], in_=total[:])
+            nc.vector.reciprocal(out=recip[head][:], in_=totals[head][:])
 
         def weighted_sum(head):
             block, b, h = place(head)
@@ -441,20 +447,27 @@ def tile_multiheadlmattentionwithcache_pa_kernel(
             if k % 2 == 1 and clock > 0:
                 quantise_weights((clock - 1) // BLOCK_STEPS + 1, ((clock - 1) % BLOCK_STEPS) // 2)
             if 0 <= k + 1 < STEPS:
-                row_maxima(k + 1)
+                bank_maxima(k + 1)
             if k % 2 == 0:
+                if 0 <= k // 2 - 2 < HEADS:
+                    row_totals(k // 2 - 2)
                 if k // 2 + 2 < HEADS:
                     transpose_keys(k // 2 + 2)
                 if clock > 0:
                     transpose_weights(clock // BLOCK_STEPS + 1, (clock % BLOCK_STEPS) // 2)
+                if 0 <= k + 1 < STEPS:
+                    negated_maximum(k + 1)
                 if 0 <= k // 2 - 2 < HEADS:
                     quantise_e(k // 2 - 2)
+                    reciprocals(k // 2 - 2)
             else:
                 if (k + 5) % BLOCK_STEPS == 0 and 0 < (k + 5) // BLOCK_STEPS < BLOCKS:
                     transpose_queries((k + 5) // BLOCK_STEPS)
                 if clock // BLOCK_STEPS < BLOCKS:
                     e, b = divmod((clock % BLOCK_STEPS) // 2, B)
                     project(clock // BLOCK_STEPS, e, b)
+                if 0 <= k + 1 < STEPS:
+                    negated_maximum(k + 1)
                 block, late = divmod(k - 3, BLOCK_STEPS)
                 if 0 <= block < BLOCKS and late in (0, 2):
                     quantise_v(block, late // 2)

@@ -161,12 +161,13 @@ def tile_multiheadlmattentionwithcache_pa_kernel(
                 codes, scales = w_codes[block]
                 quantise_rows(w_grouped[block, g], codes[:, g, :], scales[:, g, :])
 
-        def regroup_cache(block):
+        def regroup_cache(block, b):
             if block < BLOCKS:
-                grouped = work.tile([P, BLOCK_HEADS, KEY_PASSES, D, 4], BF16, align_bytes=64, name="v_grouped")
+                pair = slice(2 * b, 2 * b + 2)
+                grouped = work.tile([P, 2, KEY_PASSES, D, 4], BF16, align_bytes=64, name="v_grouped")
                 nc.gpsimd.tensor_scalar(
                     out=grouped[:, :, 0, :, :],
-                    in0=cv_raw[block][:, :, 0:2, :, :].rearrange("p n c e d -> p n d (c e)"),
+                    in0=cv_raw[block][:, pair, 0:2, :, :].rearrange("p n c e d -> p n d (c e)"),
                     scalar1=1.0,
                     scalar2=0.0,
                     op0=ALU.mult,
@@ -174,13 +175,13 @@ def tile_multiheadlmattentionwithcache_pa_kernel(
                 )
                 nc.gpsimd.tensor_scalar(
                     out=grouped[:, :, 1, :, 0:2],
-                    in0=cv_raw[block][:, :, 2, :, :].rearrange("p n e d -> p n d e"),
+                    in0=cv_raw[block][:, pair, 2, :, :].rearrange("p n e d -> p n d e"),
                     scalar1=1.0,
                     scalar2=0.0,
                     op0=ALU.mult,
                     op1=ALU.add,
                 )
-                v_grouped[block] = grouped
+                v_grouped[block, b] = grouped
 
         def project(block, e, b):
             if e == 0 and b == 0:
@@ -213,7 +214,7 @@ def tile_multiheadlmattentionwithcache_pa_kernel(
                     in_=vh[block][:, pair].rearrange("p n e d -> p n (e d)"),
                 )
                 nc.gpsimd.tensor_scalar(
-                    out=v_grouped[block][:, pair, 1, :, 2:4],
+                    out=v_grouped[block, b][:, :, 1, :, 2:4],
                     in0=vh[block][:, pair].rearrange("p n e d -> p n d e"),
                     scalar1=1.0,
                     scalar2=0.0,
@@ -231,7 +232,7 @@ def tile_multiheadlmattentionwithcache_pa_kernel(
             nc.vector.quantize_mx(
                 out=codes[:, pair].rearrange("p n g d -> p (n g d)").bitcast(FP8X4),
                 scales=scales[:, pair].rearrange("p n g d -> p (n g d)"),
-                in_=v_grouped[block][:, pair].rearrange("p n g d t -> p (n g d t)"),
+                in_=v_grouped[block, b][:].rearrange("p n g d t -> p (n g d t)"),
             )
 
         def place(head):
@@ -435,17 +436,22 @@ def tile_multiheadlmattentionwithcache_pa_kernel(
                 else:
                     w_grouped[0, g] = start_grouped[r - 1]
                     quantise_weights(0, g)
-        regroup_cache(0)
+        regroup_cache(0, 0)
+        regroup_cache(0, 1)
         transpose_queries(0)
 
         for k in range(-4, STEPS + 4):
-            clock = k + 3
             if 0 <= k < STEPS:
                 exponentials(k)
             if 0 <= k - 1 < STEPS:
                 transpose_e(k - 1)
-            if k % 2 == 1 and clock > 0:
-                quantise_weights((clock - 1) // BLOCK_STEPS + 1, ((clock - 1) % BLOCK_STEPS) // 2)
+            if k % 2 == 1:
+                if k > 0:
+                    quantise_weights((k + 7) // BLOCK_STEPS, ((k + 7) % BLOCK_STEPS) // 2)
+                pair, late = divmod(k - 3, BLOCK_STEPS // 2)
+                if late == 0 and 0 <= pair < 2 * BLOCKS:
+                    quantise_v(pair // 2, pair % 2)
+                    regroup_cache(pair // 2 + 1, pair % 2)
             if 0 <= k + 1 < STEPS:
                 bank_maxima(k + 1)
             if k % 2 == 0:
@@ -453,8 +459,8 @@ def tile_multiheadlmattentionwithcache_pa_kernel(
                     row_totals(k // 2 - 2)
                 if k // 2 + 2 < HEADS:
                     transpose_keys(k // 2 + 2)
-                if clock > 0:
-                    transpose_weights(clock // BLOCK_STEPS + 1, (clock % BLOCK_STEPS) // 2)
+                if k >= 0:
+                    transpose_weights(k // BLOCK_STEPS + 1, (k % BLOCK_STEPS) // 2)
                 if 0 <= k + 1 < STEPS:
                     negated_maximum(k + 1)
                 if 0 <= k // 2 - 2 < HEADS:
@@ -463,21 +469,17 @@ def tile_multiheadlmattentionwithcache_pa_kernel(
             else:
                 if (k + 5) % BLOCK_STEPS == 0 and 0 < (k + 5) // BLOCK_STEPS < BLOCKS:
                     transpose_queries((k + 5) // BLOCK_STEPS)
-                if clock // BLOCK_STEPS < BLOCKS:
-                    e, b = divmod((clock % BLOCK_STEPS) // 2, B)
-                    project(clock // BLOCK_STEPS, e, b)
+                if 0 <= (k + 1) // BLOCK_STEPS < BLOCKS:
+                    b, e = divmod(((k + 1) % BLOCK_STEPS) // 2, 2)
+                    project((k + 1) // BLOCK_STEPS, e, b)
                 if 0 <= k + 1 < STEPS:
                     negated_maximum(k + 1)
-                block, late = divmod(k - 3, BLOCK_STEPS)
-                if 0 <= block < BLOCKS and late in (0, 2):
-                    quantise_v(block, late // 2)
                 if 0 <= (k - 5) // 2 < HEADS:
                     weighted_sum((k - 5) // 2)
             if 0 <= k + 2 < STEPS:
                 scores(k + 2)
             if k >= 0 and k % BLOCK_STEPS == 0:
                 block = k // BLOCK_STEPS
-                regroup_cache(block + 1)
                 if block + 2 < BLOCKS:
                     load_weights(block + 2)
                     if block % 2 == 0:

@@ -51,6 +51,7 @@ def tile_multiheadlmattentionwithcache_pa_kernel(
         w_grouped, w_codes, vh, v_grouped, v_codes = {}, {}, {}, {}, {}
         qT, kT, s_banks, maxima, neg_max, e_bf, sums = {}, {}, {}, {}, {}, {}, {}
         e_grouped, e_codes, totals, recip, merged = {}, {}, {}, {}, {}
+        s_sb = {}
 
         ident_bf = consts.tile([P, P], BF16)
         make_identity(nc, ident_bf[:])
@@ -270,7 +271,7 @@ def tile_multiheadlmattentionwithcache_pa_kernel(
                     k_raw[:, i, b, first : first + D],
                     ident_bf[:],
                 )
-            kT[head] = work.tile([P, S], BF16, name="kT")
+            kT[head] = work.tile([P, S], BF16, bufs=3, name="kT")
             nc.scalar.copy(out=kT[head][:], in_=bank[:])
 
         def seen_keys(i):
@@ -309,15 +310,20 @@ def tile_multiheadlmattentionwithcache_pa_kernel(
             s_lo, s_hi = s_banks[tile]
             seen = seen_keys(tile % Q_TILES)
             maxima[tile] = small.tile([P, 2], F32, name="maxima")
-            nc.vector.tensor_reduce(out=maxima[tile][:, 0:1], in_=s_lo[:], axis=AXIS_X, op=ALU.max)
-            nc.vector.tensor_reduce(
-                out=maxima[tile][:, 1:2], in_=s_hi[:, 0 : seen - BANK], axis=AXIS_X, op=ALU.max
+            s_sb[tile] = work.tile([P, S], F32, bufs=4, name="s_sb")
+            nc.vector.tensor_scalar(
+                out=s_sb[tile][:, 0:BANK], in0=s_lo[:], scalar1=-1.0, scalar2=None,
+                op0=ALU.mult, op1=ALU.min, accum_out=maxima[tile][:, 0:1],
+            )
+            nc.vector.tensor_scalar(
+                out=s_sb[tile][:, BANK:seen], in0=s_hi[:, 0 : seen - BANK], scalar1=-1.0, scalar2=None,
+                op0=ALU.mult, op1=ALU.min, accum_out=maxima[tile][:, 1:2],
             )
 
         def negated_maximum(tile):
             neg_max[tile] = small.tile([P, 1], F32, name="neg_max")
             nc.vector.tensor_reduce(
-                out=neg_max[tile][:], in_=maxima[tile][:], axis=AXIS_X, op=ALU.max, negate=True
+                out=neg_max[tile][:], in_=maxima[tile][:], axis=AXIS_X, op=ALU.min
             )
 
         def exponentials(tile):
@@ -331,18 +337,18 @@ def tile_multiheadlmattentionwithcache_pa_kernel(
                 e_bf[tile] = work.tile([P, S], BF16, name="e_second")
             nc.scalar.activation(
                 out=e_bf[tile][:, 0:BANK],
-                in_=s_lo[:],
+                in_=s_sb[tile][:, 0:BANK],
                 func=ACT.Exp,
                 bias=neg_max[tile][:],
-                scale=1.0,
+                scale=-1.0,
                 accum_out=sums[head][:, i, 0:1],
             )
             nc.scalar.activation(
                 out=e_bf[tile][:, BANK:seen],
-                in_=s_hi[:, 0 : seen - BANK],
+                in_=s_sb[tile][:, BANK:seen],
                 func=ACT.Exp,
                 bias=neg_max[tile][:],
-                scale=1.0,
+                scale=-1.0,
                 accum_out=sums[head][:, i, 1:2],
             )
 
@@ -440,7 +446,7 @@ def tile_multiheadlmattentionwithcache_pa_kernel(
         regroup_cache(0, 1)
         transpose_queries(0)
 
-        for k in range(-4, STEPS + 4):
+        for k in range(-6, STEPS + 4):
             if 0 <= k < STEPS:
                 exponentials(k)
             if 0 <= k - 1 < STEPS:
@@ -452,32 +458,32 @@ def tile_multiheadlmattentionwithcache_pa_kernel(
                 if late == 0 and 0 <= pair < 2 * BLOCKS:
                     quantise_v(pair // 2, pair % 2)
                     regroup_cache(pair // 2 + 1, pair % 2)
-            if 0 <= k + 1 < STEPS:
-                bank_maxima(k + 1)
+            if 0 <= k + 2 < STEPS:
+                bank_maxima(k + 2)
             if k % 2 == 0:
                 if 0 <= k // 2 - 2 < HEADS:
                     row_totals(k // 2 - 2)
-                if k // 2 + 2 < HEADS:
-                    transpose_keys(k // 2 + 2)
+                if 0 <= k // 2 + 3 < HEADS:
+                    transpose_keys(k // 2 + 3)
                 if k >= 0:
                     transpose_weights(k // BLOCK_STEPS + 1, (k % BLOCK_STEPS) // 2)
-                if 0 <= k + 1 < STEPS:
-                    negated_maximum(k + 1)
+                if 0 <= k + 2 < STEPS:
+                    negated_maximum(k + 2)
                 if 0 <= k // 2 - 2 < HEADS:
                     quantise_e(k // 2 - 2)
                     reciprocals(k // 2 - 2)
             else:
-                if (k + 5) % BLOCK_STEPS == 0 and 0 < (k + 5) // BLOCK_STEPS < BLOCKS:
-                    transpose_queries((k + 5) // BLOCK_STEPS)
+                if (k + 7) % BLOCK_STEPS == 0 and 0 < (k + 7) // BLOCK_STEPS < BLOCKS:
+                    transpose_queries((k + 7) // BLOCK_STEPS)
                 if 0 <= (k + 1) // BLOCK_STEPS < BLOCKS:
                     b, e = divmod(((k + 1) % BLOCK_STEPS) // 2, 2)
                     project((k + 1) // BLOCK_STEPS, e, b)
-                if 0 <= k + 1 < STEPS:
-                    negated_maximum(k + 1)
+                if 0 <= k + 2 < STEPS:
+                    negated_maximum(k + 2)
                 if 0 <= (k - 5) // 2 < HEADS:
                     weighted_sum((k - 5) // 2)
-            if 0 <= k + 2 < STEPS:
-                scores(k + 2)
+            if 0 <= k + 3 < STEPS:
+                scores(k + 3)
             if k >= 0 and k % BLOCK_STEPS == 0:
                 block = k // BLOCK_STEPS
                 if block + 2 < BLOCKS:

@@ -50,7 +50,7 @@ def tile_multiheadlmattentionwithcache_pa_kernel(
         w_rows, qk_raw, ck_raw, cv_raw = {}, {}, {}, {}
         w_grouped, w_codes, vh, v_grouped, v_codes = {}, {}, {}, {}, {}
         qT, kT, s_banks, maxima, neg_max, e_bf, sums = {}, {}, {}, {}, {}, {}, {}
-        e_grouped, e_codes, totals, recip, merged = {}, {}, {}, {}, {}
+        e_grouped, e_codes, recip, merged = {}, {}, {}, {}
         s_sb = {}
 
         ident_bf = consts.tile([P, P], BF16)
@@ -328,28 +328,19 @@ def tile_multiheadlmattentionwithcache_pa_kernel(
 
         def exponentials(tile):
             head, i = divmod(tile, Q_TILES)
-            s_lo, s_hi = s_banks[tile]
             seen = seen_keys(i)
             if i == 0:
-                sums[head] = small.tile([P, Q_TILES, 2], F32, name="sums")
+                sums[head] = small.tile([P, Q_TILES], F32, name="sums")
                 e_bf[tile] = e_first[head % 2]
             else:
                 e_bf[tile] = work.tile([P, S], BF16, name="e_second")
             nc.scalar.activation(
-                out=e_bf[tile][:, 0:BANK],
-                in_=s_sb[tile][:, 0:BANK],
+                out=e_bf[tile][:, 0:seen],
+                in_=s_sb[tile][:, 0:seen],
                 func=ACT.Exp,
                 bias=neg_max[tile][:],
                 scale=-1.0,
-                accum_out=sums[head][:, i, 0:1],
-            )
-            nc.scalar.activation(
-                out=e_bf[tile][:, BANK:seen],
-                in_=s_sb[tile][:, BANK:seen],
-                func=ACT.Exp,
-                bias=neg_max[tile][:],
-                scale=-1.0,
-                accum_out=sums[head][:, i, 1:2],
+                accum_out=sums[head][:, i : i + 1],
             )
 
         def transpose_e(tile):
@@ -376,13 +367,9 @@ def tile_multiheadlmattentionwithcache_pa_kernel(
             )
             e_codes[head] = (codes, scales)
 
-        def row_totals(head):
-            totals[head] = small.tile([P, Q_TILES], F32, name="totals")
-            nc.vector.tensor_reduce(out=totals[head][:], in_=sums[head][:], axis=AXIS_X, op=ALU.add)
-
         def reciprocals(head):
             recip[head] = small.tile([P, Q_TILES], F32, name="recip")
-            nc.vector.reciprocal(out=recip[head][:], in_=totals[head][:])
+            nc.vector.reciprocal(out=recip[head][:], in_=sums[head][:])
 
         def weighted_sum(head):
             block, b, h = place(head)
@@ -461,8 +448,6 @@ def tile_multiheadlmattentionwithcache_pa_kernel(
             if 0 <= k + 2 < STEPS:
                 bank_maxima(k + 2)
             if k % 2 == 0:
-                if 0 <= k // 2 - 2 < HEADS:
-                    row_totals(k // 2 - 2)
                 if 0 <= k // 2 + 3 < HEADS:
                     transpose_keys(k // 2 + 3)
                 if k >= 0:

@@ -53,6 +53,10 @@ def tile_multiheadlmattentionwithcache_pa_kernel(
         e_grouped, e_codes, recip, merged = {}, {}, {}, {}
         s_sb = {}
 
+        bias_row = consts.tile([P, E], BF16)
+        nc.vector.memset(bias_row[:], 0.0)
+        ones = consts.tile([P, P], BF16)
+        nc.vector.memset(ones[:], 1.0)
         ident_bf = consts.tile([P, P], BF16)
         make_identity(nc, ident_bf[:])
         ident_f32 = consts.tile([P, P], F32)
@@ -405,16 +409,32 @@ def tile_multiheadlmattentionwithcache_pa_kernel(
                     in_=merged[block, b][:],
                 )
 
-        x_rows = [load_x(0), load_x(1)]
+        x_rows = [load_x(0)]
+        nc.sync.dma_start(out=bias_row[0:1, :], in_=bv.rearrange("(o f) -> o f", o=1))
+        x_rows.append(load_x(1))
         load_weights(0)
         load_queries_keys(0)
         load_cache(0)
-        nc.sync.dma_start(out=bias[:], in_=bv.partition_broadcast(P))
         load_weights(1)
         load_cache(1)
 
         start_grouped = {}
         for r in range(3 * PROJ_PASSES + 1):
+            if r == PROJ_PASSES:
+                for c, bank_tag in enumerate(("proj", "pv")):
+                    spread = psum.tile([P, 2 * BANK], BF16, tag=bank_tag, name="spread")
+                    for j in range(2):
+                        first = (2 * c + j) * BANK
+                        nc.tensor.matmul(
+                            spread[:, j * BANK : (j + 1) * BANK],
+                            lhsT=ones[:],
+                            rhs=bias_row[:, first : first + BANK],
+                            start=True,
+                            stop=True,
+                        )
+                    nc.vector.tensor_copy(
+                        out=bias[:, 2 * c * BANK : 2 * (c + 1) * BANK], in_=spread[:]
+                    )
             if r < 3 * PROJ_PASSES:
                 operand, g = divmod(r, PROJ_PASSES)
                 rows = x_rows[operand] if operand < 2 else w_rows[0]

@@ -51,7 +51,7 @@ def tile_multiheadlmattentionwithcache_pa_kernel(
         w_grouped, w_codes, vh, v_grouped, v_codes = {}, {}, {}, {}, {}
         qT, kT, s_banks, maxima, neg_max, e_bf, sums = {}, {}, {}, {}, {}, {}, {}
         e_grouped, e_codes, recip, merged = {}, {}, {}, {}
-        s_sb = {}
+        s_sb, pv_banks = {}, {}
 
         bias_row = consts.tile([P, E], BF16)
         nc.vector.memset(bias_row[:], 0.0)
@@ -393,6 +393,11 @@ def tile_multiheadlmattentionwithcache_pa_kernel(
                         start=(g == 0),
                         stop=(g == KEY_PASSES - 1),
                     )
+            pv_banks[head] = pv
+
+        def normalise(head):
+            block, b, h = place(head)
+            pv = pv_banks[head]
             for i in range(Q_TILES):
                 nc.scalar.activation(
                     out=merged[block, b][:, i, h * D : (h + 1) * D],
@@ -453,11 +458,13 @@ def tile_multiheadlmattentionwithcache_pa_kernel(
         regroup_cache(0, 1)
         transpose_queries(0)
 
-        for k in range(-6, STEPS + 4):
+        for k in range(-6, STEPS + 5):
             if 0 <= k < STEPS:
                 exponentials(k)
             if 0 <= k - 1 < STEPS:
                 transpose_e(k - 1)
+            if k % 2 == 0 and 0 <= (k - 6) // 2 < HEADS:
+                normalise((k - 6) // 2)
             if k % 2 == 1:
                 if k > 0:
                     quantise_weights((k + 7) // BLOCK_STEPS, ((k + 7) % BLOCK_STEPS) // 2)

from contextlib import ExitStack

import concourse.mybir as mybir
from concourse.masks import make_identity

BF16 = mybir.dt.bfloat16
F32 = mybir.dt.float32
U32 = mybir.dt.uint32
U8 = mybir.dt.uint8
FP8X4 = mybir.dt.float8_e4m3fn_x4
ALU = mybir.AluOpType
ACT = mybir.ActivationFunctionType
AXIS_X = mybir.AxisListType.X

T, B, C, E, H = 256, 2, 768, 2048, 16
D = E // H
S = C + T
NEG_INF = -10000000000.0

P = 128
K_PASS = 4 * P
PROJ_PASSES = E // K_PASS
KEY_PASSES = S // K_PASS
BANK = 512
Q_TILES = T // P
CACHE_TILES = C // P
BLOCK_FEATS = 2 * D
BLOCKS = E // BLOCK_FEATS
BLOCK_HEADS = 2 * B
HEADS = BLOCKS * BLOCK_HEADS
STEPS = HEADS * Q_TILES
BLOCK_STEPS = BLOCK_HEADS * Q_TILES

FLOPS = 2 * T * B * E * E + 2 * 2 * B * H * T * S * D


def tile_multiheadlmattentionwithcache_pa_kernel(
    tc, x, q, k_new, cache_k, cache_v, Wv, bv, out_0, out_1
):
    nc = tc.nc
    with ExitStack() as ctx:
        consts = ctx.enter_context(tc.tile_pool(name="consts", bufs=1))
        loads = ctx.enter_context(tc.tile_pool(name="loads", bufs=3))
        work = ctx.enter_context(tc.tile_pool(name="work", bufs=2))
        small = ctx.enter_context(tc.tile_pool(name="small", bufs=4))
        psum = ctx.enter_context(tc.psum_pool(name="psum", bufs=1))
        psum_s = ctx.enter_context(tc.psum_pool(name="psum_s", bufs=2))
        ctx.enter_context(tc.manual_schedule())

        w_rows, qk_raw, ck_raw, cv_raw = {}, {}, {}, {}
        w_grouped, w_codes, vh, v_grouped, v_codes = {}, {}, {}, {}, {}
        qT, kT, s_banks, maxima, neg_max, e_bf, sums = {}, {}, {}, {}, {}, {}, {}
        e_grouped, e_codes, recip, merged = {}, {}, {}, {}
        s_sb, pv_banks = {}, {}

        bias_row = consts.tile([P, E], BF16)
        nc.vector.memset(bias_row[:], 0.0)
        ones = consts.tile([P, P], BF16)
        nc.vector.memset(ones[:], 1.0)
        ident_bf = consts.tile([P, P], BF16)
        make_identity(nc, ident_bf[:])
        ident_f32 = consts.tile([P, P], F32)
        make_identity(nc, ident_f32[:])
        mask_f32 = consts.tile([P, P], F32)
        nc.gpsimd.memset(mask_f32[:], 0.0)
        nc.gpsimd.affine_select(
            out=mask_f32[:],
            in_=mask_f32[:],
            compare_op=ALU.is_ge,
            fill=NEG_INF,
            base=0,
            pattern=[[-1, P]],
            channel_multiplier=1,
        )
        mask_bf = consts.tile([P, P], BF16)
        nc.vector.tensor_copy(out=mask_bf[:], in_=mask_f32[:])
        e_first = [consts.tile([P, S], BF16, name="e_first%d" % j) for j in range(2)]
        for j in range(2):
            nc.vector.memset(e_first[j][:, S - P : S], 0.0)
        bias = consts.tile([P, E], BF16)
        x_codes = consts.tile([P, PROJ_PASSES, 4 * P], U32, align_bytes=64)
        x_scales = consts.tile([P, PROJ_PASSES, 4 * P], U8, align_bytes=64)

        def load_x(pair):
            rows = loads.tile([P, 2, E], BF16, tag="rows", bufs=4, name="x_rows")
            nc.sync.dma_start(
                out=rows[:].rearrange("p b k -> p (b k)"),
                in_=x.rearrange("(p e) b k -> e p (b k)", e=2)[pair],
            )
            return rows

        def load_weights(block):
            first = block * BLOCK_FEATS
            rows = loads.tile([P, 2, E], BF16, tag="rows", bufs=4, name="w_rows")
            nc.sync.dma_start(
                out=rows[:],
                in_=Wv[first : first + BLOCK_FEATS, :].rearrange("(r p) k -> p r k", p=P),
            )
            w_rows[block] = rows

        def load_queries_keys(two_blocks):
            feats = slice(two_blocks * BANK, (two_blocks + 1) * BANK)
            q_raw = loads.tile([P, Q_TILES, B, BANK], BF16, bufs=2, name="q_raw")
            k_raw = loads.tile([P, Q_TILES, B, BANK], BF16, bufs=2, name="k_raw")
            for i in range(Q_TILES):
                rows = slice(i * P, (i + 1) * P)
                nc.sync.dma_start(out=q_raw[:, i], in_=q[rows, :, feats])
                nc.sync.dma_start(out=k_raw[:, i], in_=k_new[rows, :, feats])
            qk_raw[two_blocks] = (q_raw, k_raw)

        def load_cache(block):
            ck = loads.tile([P, BLOCK_HEADS, CACHE_TILES, D], BF16, name="ck")
            cv = loads.tile([P, BLOCK_HEADS, 3, 2, D], BF16, name="cv")
            for b in range(B):
                n0 = b * H + 2 * block
                nc.sync.dma_start(
                    out=ck[:, 2 * b : 2 * b + 2].rearrange("p n a d -> p (n a) d"),
                    in_=cache_k[n0 : n0 + 2].rearrange("n (a p) d -> p (n a) d", p=P),
                )
            for b in range(B):
                n0 = b * H + 2 * block
                nc.sync.dma_start(
                    out=cv[:, 2 * b : 2 * b + 2].rearrange("p n c e d -> p (n c) (e d)"),
                    in_=cache_v[n0 : n0 + 2].rearrange("n (c p e) d -> p (n c) (e d)", c=3, e=2),
                )
            ck_raw[block] = ck
            cv_raw[block] = cv

        def transpose_rows(rows, g, bank_pool, bank_tag, copy_out):
            words = (
                rows[:]
                .rearrange("p r k -> p (r k)")
                .bitcast(F32)
                .rearrange("p (r w) -> p r w", r=2)
            )
            bank = bank_pool.tile([P, 2, 2, P], F32, tag=bank_tag, name="rows_T")
            for r in range(2):
                for u in range(2):
                    first = (2 * g + u) * P
                    nc.tensor.transpose(bank[:, r, u, :], words[:, r, first : first + P], ident_f32[:])
            grouped = work.tile(
                [P, 2, P, 2], F32, tag="rows_grouped", bufs=3, align_bytes=64, name="rows_grouped"
            )
            copy_out(out=grouped[:], in_=bank[:].rearrange("p r u c -> p r c u"))
            return grouped

        def quantise_rows(grouped, codes, scales):
            nc.vector.quantize_mx(
                out=codes.bitcast(FP8X4),
                scales=scales,
                in_=grouped[:].rearrange("p r c u -> p (r c u)").bitcast(BF16),
            )

        def transpose_weights(block, g):
            if block < BLOCKS:
                w_grouped[block, g] = transpose_rows(
                    w_rows[block], g, psum, "proj", nc.vector.tensor_copy
                )

        def quantise_weights(block, g):
            if block < BLOCKS:
                if g == 0:
                    codes = work.tile([P, PROJ_PASSES, BLOCK_FEATS], U32, align_bytes=64, name="w_codes")
                    scales = work.tile([P, PROJ_PASSES, BLOCK_FEATS], U8, align_bytes=64, name="w_scales")
                    w_codes[block] = (codes, scales)
                codes, scales = w_codes[block]
                quantise_rows(w_grouped[block, g], codes[:, g, :], scales[:, g, :])

        def regroup_cache(block, b):
            if block < BLOCKS:
                pair = slice(2 * b, 2 * b + 2)
                grouped = work.tile([P, 2, KEY_PASSES, D, 4], BF16, align_bytes=64, name="v_grouped")
                nc.gpsimd.tensor_scalar(
                    out=grouped[:, :, 0, :, :],
                    in0=cv_raw[block][:, pair, 0:2, :, :].rearrange("p n c e d -> p n d (c e)"),
                    scalar1=1.0,
                    scalar2=0.0,
                    op0=ALU.mult,
                    op1=ALU.add,
                )
                nc.gpsimd.tensor_scalar(
                    out=grouped[:, :, 1, :, 0:2],
                    in0=cv_raw[block][:, pair, 2, :, :].rearrange("p n e d -> p n d e"),
                    scalar1=1.0,
                    scalar2=0.0,
                    op0=ALU.mult,
                    op1=ALU.add,
                )
                v_grouped[block, b] = grouped

        def project(block, e, b):
            if e == 0 and b == 0:
                vh[block] = work.tile([P, BLOCK_HEADS, 2, D], F32, name="vh")
            codes, scales = w_codes[block]
            tokens = slice((2 * e + b) * P, (2 * e + b + 1) * P)
            first = block * BLOCK_FEATS
            acc = psum.tile([P, BLOCK_FEATS], F32, tag="proj", name="acc")
            for g in range(PROJ_PASSES):
                nc.tensor.matmul_mx(
                    out=acc[:],
                    lhsT=x_codes[:, g, tokens].bitcast(FP8X4),
                    lhsT_scale=x_scales[:, g, tokens],
                    rhs=codes[:, g, :].bitcast(FP8X4),
                    rhs_scale=scales[:, g, :],
                    start=(g == 0),
                    stop=(g == PROJ_PASSES - 1),
                )
            pair = slice(2 * b, 2 * b + 2)
            nc.vector.tensor_tensor(
                out=vh[block][:, pair, e, :],
                in0=acc[:].rearrange("p (n d) -> p n d", d=D),
                in1=bias[:, first : first + BLOCK_FEATS].rearrange("p (n d) -> p n d", d=D),
                op=ALU.add,
            )
            if e == 1:
                n0 = b * H + 2 * block
                nc.sync.dma_start(
                    out=out_1[n0 : n0 + 2].rearrange("n (p e) d -> p n (e d)", e=2),
                    in_=vh[block][:, pair].rearrange("p n e d -> p n (e d)"),
                )
                nc.gpsimd.tensor_scalar(
                    out=v_grouped[block, b][:, :, 1, :, 2:4],
                    in0=vh[block][:, pair].rearrange("p n e d -> p n d e"),
                    scalar1=1.0,
                    scalar2=0.0,
                    op0=ALU.mult,
                    op1=ALU.add,
                )

        def quantise_v(block, b):
            if b == 0:
                codes = work.tile([P, BLOCK_HEADS, KEY_PASSES, D], U32, align_bytes=64, name="v_codes")
                scales = work.tile([P, BLOCK_HEADS, KEY_PASSES, D], U8, align_bytes=64, name="v_scales")
                v_codes[block] = (codes, scales)
            codes, scales = v_codes[block]
            pair = slice(2 * b, 2 * b + 2)
            nc.vector.quantize_mx(
                out=codes[:, pair].rearrange("p n g d -> p (n g d)").bitcast(FP8X4),
                scales=scales[:, pair].rearrange("p n g d -> p (n g d)"),
                in_=v_grouped[block, b][:].rearrange("p n g d t -> p (n g d t)"),
            )

        def place(head):
            block, rest = divmod(head, BLOCK_HEADS)
            b, h = divmod(rest, 2)
            return block, b, h

        def transpose_queries(block):
            q_raw = qk_raw[block // 2][0]
            bank = psum.tile([P, BLOCK_HEADS, T], BF16, tag="kq", name="qT_ps")
            for b in range(B):
                for h in range(2):
                    first = ((block % 2) * 2 + h) * D
                    for i in range(Q_TILES):
                        nc.tensor.transpose(
                            bank[:, 2 * b + h, i * P : (i + 1) * P],
                            q_raw[:, i, b, first : first + D],
                            ident_bf[:],
                        )
            qT[block] = work.tile([P, BLOCK_HEADS, T], BF16, name="qT")
            nc.scalar.copy(out=qT[block][:], in_=bank[:])

        def transpose_keys(head):
            block, b, h = place(head)
            k_raw = qk_raw[block // 2][1]
            first = ((block % 2) * 2 + h) * D
            bank = psum.tile([P, S], BF16, tag="kq", name="kT_ps")
            for a in range(CACHE_TILES):
                nc.tensor.transpose(
                    bank[:, a * P : (a + 1) * P], ck_raw[block][:, 2 * b + h, a, :], ident_bf[:]
                )
            for i in range(Q_TILES):
                nc.tensor.transpose(
                    bank[:, C + i * P : C + (i + 1) * P],
                    k_raw[:, i, b, first : first + D],
                    ident_bf[:],
                )
            kT[head] = work.tile([P, S], BF16, bufs=3, name="kT")
            nc.scalar.copy(out=kT[head][:], in_=bank[:])

        def seen_keys(i):
            return C + (i + 1) * P

        def scores(tile):
            head, i = divmod(tile, Q_TILES)
            block, b, h = place(head)
            queries = qT[block][:, 2 * b + h, i * P : (i + 1) * P]
            keys = kT[head]
            seen = seen_keys(i)
            diag = seen - P
            s_lo = psum_s.tile([P, BANK], F32, tag="s_lo", name="s_lo")
            s_hi = psum_s.tile([P, BANK], F32, tag="s_hi", name="s_hi")
            nc.tensor.matmul(s_lo[:], lhsT=queries, rhs=keys[:, 0:BANK], start=True, stop=True)
            nc.tensor.matmul(
                s_hi[:, 0 : diag - BANK], lhsT=queries, rhs=keys[:, BANK:diag], start=True, stop=True
            )
            nc.tensor.matmul(
                s_hi[:, diag - BANK : seen - BANK],
                lhsT=queries,
                rhs=keys[:, diag:seen],
                start=True,
                stop=False,
            )
            nc.tensor.matmul(
                s_hi[:, diag - BANK : seen - BANK],
                lhsT=ident_bf[:],
                rhs=mask_bf[:],
                start=False,
                stop=True,
            )
            s_banks[tile] = (s_lo, s_hi)

        def bank_maxima(tile):
            s_lo, s_hi = s_banks[tile]
            seen = seen_keys(tile % Q_TILES)
            maxima[tile] = small.tile([P, 2], F32, name="maxima")
            s_sb[tile] = work.tile([P, S], F32, bufs=4, name="s_sb")
            nc.vector.tensor_scalar(
                out=s_sb[tile][:, 0:BANK], in0=s_lo[:], scalar1=-1.0, scalar2=None,
                op0=ALU.mult, op1=ALU.min, accum_out=maxima[tile][:, 0:1],
            )
            nc.vector.tensor_scalar(
                out=s_sb[tile][:, BANK:seen], in0=s_hi[:, 0 : seen - BANK], scalar1=-1.0, scalar2=None,
                op0=ALU.mult, op1=ALU.min, accum_out=maxima[tile][:, 1:2],
            )

        def negated_maximum(tile):
            neg_max[tile] = small.tile([P, 1], F32, name="neg_max")
            nc.vector.tensor_reduce(
                out=neg_max[tile][:], in_=maxima[tile][:], axis=AXIS_X, op=ALU.min
            )

        def exponentials(tile):
            head, i = divmod(tile, Q_TILES)
            seen = seen_keys(i)
            if i == 0:
                sums[head] = small.tile([P, Q_TILES], F32, name="sums")
                e_bf[tile] = e_first[head % 2]
            else:
                e_bf[tile] = work.tile([P, S], BF16, name="e_second")
            nc.scalar.activation(
                out=e_bf[tile][:, 0:seen],
                in_=s_sb[tile][:, 0:seen],
                func=ACT.Exp,
                bias=neg_max[tile][:],
                scale=-1.0,
                accum_out=sums[head][:, i : i + 1],
            )

        def transpose_e(tile):
            head, i = divmod(tile, Q_TILES)
            if i == 0:
                e_grouped[head] = work.tile(
                    [P, Q_TILES, KEY_PASSES, P, 2], F32, bufs=3, align_bytes=64, name="e_grouped"
                )
            e_words = e_bf[tile][:].bitcast(F32)
            bank = psum.tile([P, 2 * KEY_PASSES, P], F32, tag="eT", name="eT_ps")
            for w in range(2 * KEY_PASSES):
                nc.tensor.transpose(bank[:, w, :], e_words[:, w * P : (w + 1) * P], ident_f32[:])
            nc.scalar.copy(
                out=e_grouped[head][:, i], in_=bank[:].rearrange("p (g u) c -> p g c u", u=2)
            )

        def quantise_e(head):
            codes = work.tile([P, Q_TILES, KEY_PASSES, P], U32, align_bytes=64, name="e_codes")
            scales = work.tile([P, Q_TILES, KEY_PASSES, P], U8, align_bytes=64, name="e_scales")
            nc.vector.quantize_mx(
                out=codes[:].rearrange("p i g c -> p (i g c)").bitcast(FP8X4),
                scales=scales[:].rearrange("p i g c -> p (i g c)"),
                in_=e_grouped[head][:].rearrange("p i g c u -> p (i g c u)").bitcast(BF16),
            )
            e_codes[head] = (codes, scales)

        def reciprocals(head):
            recip[head] = small.tile([P, Q_TILES], F32, name="recip")
            nc.vector.reciprocal(out=recip[head][:], in_=sums[head][:])

        def weighted_sum(head):
            block, b, h = place(head)
            if h == 0:
                merged[block, b] = work.tile([P, Q_TILES, BLOCK_FEATS], F32, name="merged")
            codes, scales = e_codes[head]
            values, value_scales = v_codes[block]
            pv = psum.tile([P, Q_TILES, D], F32, tag="pv", name="pv")
            for i in range(Q_TILES):
                for g in range(KEY_PASSES):
                    nc.tensor.matmul_mx(
                        out=pv[:, i, :],
                        lhsT=codes[:, i, g, :].bitcast(FP8X4),
                        lhsT_scale=scales[:, i, g, :],
                        rhs=values[:, 2 * b + h, g, :].bitcast(FP8X4),
                        rhs_scale=value_scales[:, 2 * b + h, g, :],
                        start=(g == 0),
                        stop=(g == KEY_PASSES - 1),
                    )
            pv_banks[head] = pv

        def normalise(head):
            block, b, h = place(head)
            pv = pv_banks[head]
            for i in range(Q_TILES):
                nc.scalar.activation(
                    out=merged[block, b][:, i, h * D : (h + 1) * D],
                    in_=pv[:, i, :],
                    func=ACT.Copy,
                    scale=recip[head][:, i : i + 1],
                )
            if h == 1:
                first = block * BLOCK_FEATS
                nc.sync.dma_start(
                    out=out_0.rearrange("(i p) b f -> p i b f", p=P)[
                        :, :, b, first : first + BLOCK_FEATS
                    ],
                    in_=merged[block, b][:],
                )

        x_rows = [load_x(0)]
        nc.sync.dma_start(out=bias_row[0:1, :], in_=bv.rearrange("(o f) -> o f", o=1))
        x_rows.append(load_x(1))
        load_weights(0)
        load_queries_keys(0)
        load_cache(0)
        load_weights(1)
        load_cache(1)

        start_grouped = {}
        for r in range(3 * PROJ_PASSES + 1):
            if r == PROJ_PASSES:
                for c, bank_tag in enumerate(("proj", "pv")):
                    spread = psum.tile([P, 2 * BANK], BF16, tag=bank_tag, name="spread")
                    for j in range(2):
                        first = (2 * c + j) * BANK
                        nc.tensor.matmul(
                            spread[:, j * BANK : (j + 1) * BANK],
                            lhsT=ones[:],
                            rhs=bias_row[:, first : first + BANK],
                            start=True,
                            stop=True,
                        )
                    nc.vector.tensor_copy(
                        out=bias[:, 2 * c * BANK : 2 * (c + 1) * BANK], in_=spread[:]
                    )
            if r < 3 * PROJ_PASSES:
                operand, g = divmod(r, PROJ_PASSES)
                rows = x_rows[operand] if operand < 2 else w_rows[0]
                start_grouped[r] = transpose_rows(
                    rows, g, psum_s, ("s_lo", "s_hi")[r % 2], nc.scalar.copy
                )
            if r > 0:
                operand, g = divmod(r - 1, PROJ_PASSES)
                if operand < 2:
                    tokens = slice(operand * 2 * P, (operand + 1) * 2 * P)
                    quantise_rows(start_grouped[r - 1], x_codes[:, g, tokens], x_scales[:, g, tokens])
                else:
                    w_grouped[0, g] = start_grouped[r - 1]
                    quantise_weights(0, g)
        regroup_cache(0, 0)
        regroup_cache(0, 1)
        transpose_queries(0)

        for k in range(-6, STEPS + 5):
            if 0 <= k < STEPS:
                exponentials(k)
            if 0 <= k - 1 < STEPS:
                transpose_e(k - 1)
            if k % 2 == 0 and 0 <= (k - 6) // 2 < HEADS:
                normalise((k - 6) // 2)
            if k % 2 == 1:
                if k > 0:
                    quantise_weights((k + 7) // BLOCK_STEPS, ((k + 7) % BLOCK_STEPS) // 2)
                pair, late = divmod(k - 3, BLOCK_STEPS // 2)
                if late == 0 and 0 <= pair < 2 * BLOCKS:
                    quantise_v(pair // 2, pair % 2)
                    regroup_cache(pair // 2 + 1, pair % 2)
            if 0 <= k + 2 < STEPS:
                bank_maxima(k + 2)
            if k % 2 == 0:
                if 0 <= k // 2 + 3 < HEADS:
                    transpose_keys(k // 2 + 3)
                if k >= 0:
                    transpose_weights(k // BLOCK_STEPS + 1, (k % BLOCK_STEPS) // 2)
                if 0 <= k + 2 < STEPS:
                    negated_maximum(k + 2)
                if 0 <= k // 2 - 2 < HEADS:
                    quantise_e(k // 2 - 2)
                    reciprocals(k // 2 - 2)
            else:
                if (k + 7) % BLOCK_STEPS == 0 and 0 < (k + 7) // BLOCK_STEPS < BLOCKS:
                    transpose_queries((k + 7) // BLOCK_STEPS)
                if 0 <= (k + 1) // BLOCK_STEPS < BLOCKS:
                    b, e = divmod(((k + 1) % BLOCK_STEPS) // 2, 2)
                    project((k + 1) // BLOCK_STEPS, e, b)
                if 0 <= k + 2 < STEPS:
                    negated_maximum(k + 2)
                if 0 <= (k - 5) // 2 < HEADS:
                    weighted_sum((k - 5) // 2)
            if 0 <= k + 3 < STEPS:
                scores(k + 3)
            if k >= 0 and k % BLOCK_STEPS == 0:
                block = k // BLOCK_STEPS
                if block + 2 < BLOCKS:
                    load_weights(block + 2)
                    if block % 2 == 0:
                        load_queries_keys(block // 2 + 1)
                    load_cache(block + 2)
